import numpy as np
import ml_dtypes


def mxq(x, axis, fmt="e4m3"):
    dtype, down = {"e4m3": (ml_dtypes.float8_e4m3fn, 7), "e5m2": (ml_dtypes.float8_e5m2, 14)}[fmt]
    v = np.moveaxis(np.asarray(x, np.float32).astype(ml_dtypes.bfloat16).astype(np.float64), axis, -1)
    blocks = v.reshape(v.shape[:-1] + (-1, 32))
    amax = np.abs(blocks).max(-1, keepdims=True)
    byte = np.maximum(np.where(amax > 0, np.frexp(amax)[1] - 1 + 127, 0) - down, 1)
    scale = np.exp2(byte - 127.0)
    codes = (blocks / scale).astype(np.float32).astype(dtype).astype(np.float64)
    return np.moveaxis((codes * scale).reshape(v.shape), -1, axis)


WIDE = False


def mx_kscale(k):
    if not WIDE:
        return np.ones(k)
    levels = np.array([10, -10, 5, -5, 0])
    if k % 512:
        return np.exp2(np.random.permutation(np.resize(levels, k // 32))).repeat(32)
    a = np.empty((k // 512, 16))
    for p in range(k // 512):
        a[p, :8] = np.random.permutation(np.resize(levels, 8))
        for g in range(8):
            far = levels[np.abs(levels - a[p, g]) >= 10]
            a[p, g + 8] = far[np.random.randint(len(far))]
    return np.exp2(a.ravel()).repeat(32)


BF16 = ml_dtypes.bfloat16


def bf(x):
    return np.asarray(x, np.float32).astype(BF16)


def f64(x):
    return np.asarray(x).astype(np.float64)


S, D = 512, 2048
HALF = D // 2
BASE = 10000.0


def rope_interleaved(v):
    freqs = 1.0 / BASE ** (np.arange(HALF) / HALF)
    ang = np.arange(S)[:, None] * freqs[None, :]
    cos, sin = np.cos(ang), np.sin(ang)
    vp = v.reshape(S, HALF, 2)
    vr, vi = vp[..., 0], vp[..., 1]
    rot = np.stack([vr * cos - vi * sin, vr * sin + vi * cos], axis=-1)
    return rot.reshape(S, D)


def setup_inputs():
    s = mx_kscale(D)
    return {"x": bf(np.random.standard_normal((S, D)) * s),
            "w": bf(np.random.standard_normal((D, D)) / np.sqrt(D) / s[None, :])}


def reference(x, w):
    y = mxq(f64(x), 1, "e4m3") @ mxq(f64(w), 1, "e4m3").T
    return rope_interleaved(y)

@@ -1,0 +1,228 @@
+import math
+from contextlib import ExitStack
+
+import concourse.mybir as mybir
+from concourse.masks import make_identity
+
+F32 = mybir.dt.float32
+BF16 = mybir.dt.bfloat16
+I32 = mybir.dt.int32
+U32 = mybir.dt.uint32
+U8 = mybir.dt.uint8
+FP8X4 = mybir.dt.float8_e4m3fn_x4
+ALU = mybir.AluOpType
+ACT = mybir.ActivationFunctionType
+
+P = 128
+S, D = 512, 2048
+HALF = D // 2
+BASE = 10000.0
+FLOPS = 2 * S * D * D
+
+NT = S // P
+NG = D // 512
+NU = 8
+TWO_PI = 2.0 * math.pi
+THR = (496, 576)
+CHUNKS = (3, 2, 1, 0)
+X_EVAC = ("s", "s")
+HEAD = 0
+W_EVAC_V = 2
+LAST_ON_VECTOR = 2
+
+
+def tile_ropeattention_pa_kernel(tc, x, w, out):
+    nc = tc.nc
+    with ExitStack() as ctx:
+        const = ctx.enter_context(tc.tile_pool(name="const", bufs=1))
+        big = ctx.enter_context(tc.tile_pool(name="big", bufs=1))
+        grp = ctx.enter_context(tc.tile_pool(name="grp", bufs=5))
+        codes = ctx.enter_context(tc.tile_pool(name="codes", bufs=3))
+        work = ctx.enter_context(tc.tile_pool(name="work", bufs=3))
+        psum = ctx.enter_context(tc.psum_pool(name="psum", bufs=4))
+
+        x_sb = [big.tile([P, D], BF16, name="x_sb%d" % t) for t in range(NT)]
+        w_sb = [big.tile([P, 2 * D], BF16, name="w_sb%d" % k) for k in range(NU)]
+
+        def load_x(t):
+            nc.sync.dma_start(out=x_sb[t][:], in_=x[t * P:(t + 1) * P, :])
+
+        def load_w(k):
+            n, e = CHUNKS[k // 2], k % 2
+            rows = w[n * 512:(n + 1) * 512, :].rearrange("(a p e) k -> e p a k", a=2, e=2)
+            nc.sync.dma_start(out=w_sb[k][:].rearrange("p (a k) -> p a k", a=2), in_=rows[e])
+
+        load_x(0)
+        load_w(0)
+        for t in range(1, NT):
+            load_x(t)
+        for k in range(1, NU):
+            load_w(k)
+
+        warm = const.tile([P, 2], F32, name="warm")
+        nc.vector.memset(warm[:, 0:1], 0.0)
+        nc.scalar.activation(out=warm[:, 1:2], in_=warm[:, 0:1], func=ACT.Sin)
+        ident = const.tile([P, P], F32, name="ident")
+        make_identity(nc, ident[:])
+        s_int = const.tile([P, NT], I32, name="s_int")
+        nc.gpsimd.iota(s_int[:], pattern=[[P, NT]], base=0, channel_multiplier=1)
+        sc = const.tile([P, 16], F32, name="sc")
+        nc.vector.tensor_copy(out=sc[:, 0:4], in_=s_int[:])
+        nc.vector.tensor_scalar(out=sc[:, 4:8], in0=sc[:, 0:4], scalar1=-1.0, scalar2=None, op0=ALU.mult)
+        nc.vector.tensor_scalar(out=sc[:, 8:12], in0=sc[:, 0:4], scalar1=1.0 / TWO_PI, scalar2=None, op0=ALU.mult)
+        nc.vector.memset(sc[:, 12:13], 1.0)
+        nc.vector.tensor_scalar(out=sc[:, 13:14], in0=sc[:, 12:13], scalar1=0.5 * math.pi, scalar2=None, op0=ALU.mult)
+        half_pi = sc[:, 13:14]
+
+        freq = const.tile([P, HALF], F32, name="freq")
+        nc.vector.memset(freq[:, 0:1], 1.0)
+        size = 1
+        while size < HALF:
+            for m in range(1, 4):
+                nc.vector.tensor_scalar(
+                    out=freq[:, m * size:(m + 1) * size], in0=freq[:, 0:size],
+                    scalar1=BASE ** (-(m * size) / HALF), scalar2=None, op0=ALU.mult,
+                )
+            size *= 4
+
+        frac = [const.tile([P, 2, THR[tp]], F32, name="frac%d" % tp) for tp in range(2)]
+        afr = [const.tile([P, 2, THR[tp]], F32, name="afr%d" % tp) for tp in range(2)]
+        tab = [const.tile([P, NT, 3, 256], F32, name="tab%d" % n) for n in range(4)]
+
+        def reduce_turns(t):
+            hi = THR[t // 2]
+            turns = work.tile([P, 576], U32, name="turns", bufs=2)
+            nc.scalar.activation(out=turns[:, 0:hi], in_=freq[:, 0:hi], func=ACT.Copy, scale=sc[:, 8 + t:9 + t])
+            nc.vector.scalar_tensor_tensor(out=frac[t // 2][:, t % 2, :], in0=freq[:, 0:hi], scalar=sc[:, 8 + t:9 + t],
+                                           in1=turns[:, 0:hi].bitcast(I32), op0=ALU.mult, op1=ALU.subtract)
+
+        def tables_half(c, tp):
+            if c >= len(CHUNKS):
+                return
+            n = CHUNKS[c]
+            lo, hi = 256 * n, 256 * (n + 1)
+            mid = min(max(THR[tp], lo), hi)
+            both = slice(2 * tp, 2 * tp + 2)
+            if mid > lo:
+                nc.scalar.activation(out=afr[tp][:, :, lo:mid], in_=frac[tp][:, :, lo:mid], func=ACT.Abs)
+                nc.scalar.activation(out=tab[n][:, both, 2, 0:mid - lo], in_=frac[tp][:, :, lo:mid], func=ACT.Sin,
+                                     scale=TWO_PI)
+                nc.scalar.activation(out=tab[n][:, both, 1, 0:mid - lo], in_=afr[tp][:, :, lo:mid], func=ACT.Sin,
+                                     scale=-TWO_PI, bias=half_pi)
+            if mid < hi:
+                for t in (2 * tp, 2 * tp + 1):
+                    nc.scalar.activation(out=tab[n][:, t, 2, mid - lo:256], in_=freq[:, mid:hi], func=ACT.Sin,
+                                         scale=sc[:, t:t + 1])
+                    nc.scalar.activation(out=tab[n][:, t, 1, mid - lo:256], in_=freq[:, mid:hi], func=ACT.Sin,
+                                         scale=sc[:, 4 + t:5 + t], bias=half_pi)
+            nc.gpsimd.tensor_scalar(out=tab[n][:, both, 0, :], in0=tab[n][:, both, 2, :],
+                                    scalar1=-1.0, scalar2=0.0, op0=ALU.mult, op1=ALU.add)
+
+        x_codes = [big.tile([P, 512], U32, name="x_codes%d" % t, align_bytes=64) for t in range(NT)]
+        x_scale = [big.tile([P, 512], U8, name="x_scale%d" % t, align_bytes=64) for t in range(NT)]
+
+        def x_tile(t):
+            xw = x_sb[t][:].bitcast(F32)
+            g4 = grp.tile([P, 2048], BF16, name="g4", align_bytes=64)
+            g4w = g4[:].bitcast(F32)
+            for b in range(2):
+                bank = psum.tile([P, 512], F32, name="tp")
+                for gl in range(2):
+                    for u in range(2):
+                        g = 2 * b + gl
+                        nc.tensor.transpose(bank[:, (2 * gl + u) * P:(2 * gl + u + 1) * P],
+                                            xw[:, g * 2 * P + u:(g + 1) * 2 * P:2], ident[:])
+                dst = g4w[:, b * 512:(b + 1) * 512].rearrange("p (g r u) -> p g r u", g=2, u=2)
+                src = bank[:].rearrange("p (g u r) -> p g r u", g=2, u=2)
+                if X_EVAC[b] == "v":
+                    nc.vector.tensor_copy(out=dst, in_=src)
+                else:
+                    nc.scalar.copy(out=dst, in_=src)
+            nc.vector.quantize_mx(out=x_codes[t][:].bitcast(FP8X4), scales=x_scale[t][:], in_=g4[:])
+
+        w_codes = {}
+        w_scale = {}
+
+        def w_unit(k):
+            ww = w_sb[k][:].bitcast(F32)
+            w_codes[k] = codes.tile([P, 1024], U32, name="w_codes", align_bytes=64)
+            w_scale[k] = codes.tile([P, 1024], U8, name="w_scale", align_bytes=64)
+            for h in range(2):
+                g4 = grp.tile([P, 2048], BF16, name="g4", align_bytes=64)
+                g4w = g4[:].bitcast(F32)
+                for gl in range(2):
+                    g = 2 * h + gl
+                    bank = psum.tile([P, 512], F32, name="tp")
+                    for u in range(2):
+                        for e in range(2):
+                            c0 = e * 1024 + g * 2 * P
+                            nc.tensor.transpose(bank[:, (2 * u + e) * P:(2 * u + e + 1) * P],
+                                                ww[:, c0 + u:c0 + 2 * P:2], ident[:])
+                    dst = g4w[:, gl * 512:(gl + 1) * 512].rearrange("p (c u) -> p c u", u=2)
+                    src = bank[:].rearrange("p (u c) -> p c u", u=2)
+                    if k < W_EVAC_V and gl == 1:
+                        nc.vector.tensor_copy(out=dst, in_=src)
+                    else:
+                        nc.scalar.copy(out=dst, in_=src)
+                nc.vector.quantize_mx(out=w_codes[k][:, h * 512:(h + 1) * 512].bitcast(FP8X4),
+                                      scales=w_scale[k][:, h * 512:(h + 1) * 512], in_=g4[:])
+
+        first_products = {}
+
+        def mx_unit(k):
+            n, e = CHUNKS[k // 2], k % 2
+            last = k == NU - 1
+            groups = [(t,) for t in range(NT)] if last else [(0, 1), (2, 3)]
+            for tiles in groups:
+                nt = len(tiles)
+                y = psum.tile([P, 512], F32, name="tp" if last else "y")
+                for j, t in enumerate(tiles):
+                    for g in range(NG):
+                        nc.tensor.matmul_mx(
+                            out=y[:, j * 256:(j + 1) * 256],
+                            lhsT=x_codes[t][:, g * P:(g + 1) * P].bitcast(FP8X4),
+                            lhsT_scale=x_scale[t][:, g * P:(g + 1) * P],
+                            rhs=w_codes[k][:, g * 256:(g + 1) * 256].bitcast(FP8X4),
+                            rhs_scale=w_scale[k][:, g * 256:(g + 1) * 256],
+                            start=(g == 0), stop=(g == NG - 1),
+                        )
+                prod = work.tile([P, 2, 256, 2], F32, name="pa" if e == 0 else "pb", bufs=4 if e == 0 else 3)
+                nc.vector.tensor_tensor(
+                    out=prod[:, 0:nt],
+                    in0=y[:, 0:nt * 256].rearrange("p (t r) -> p t r", t=nt).unsqueeze(3).to_broadcast([P, nt, 256, 2]),
+                    in1=tab[n][:, tiles[0]:tiles[0] + nt, 1 - e:3 - e, :].rearrange("p t c r -> p t r c"),
+                    op=ALU.mult,
+                )
+                if e == 0:
+                    first_products[tiles[0] // 2] = prod
+                else:
+                    eng = nc.vector if (last and tiles[0] >= LAST_ON_VECTOR) else nc.gpsimd
+                    for j, t in enumerate(tiles):
+                        res = first_products[t // 2][:, t % 2]
+                        eng.tensor_tensor(out=res, in0=res, in1=prod[:, j], op=ALU.add)
+                        nc.sync.dma_start(out=out[t * P:(t + 1) * P, n * 512:(n + 1) * 512],
+                                          in_=res.rearrange("p r c -> p (r c)"))
+
+        for t in range(NT):
+            reduce_turns(t)
+        if HEAD == 0:
+            x_tile(0)
+            w_unit(0)
+            for t in range(1, NT):
+                x_tile(t)
+            tables_half(0, 0)
+            tables_half(0, 1)
+        elif HEAD == 1:
+            tables_half(0, 0)
+            x_tile(0)
+            w_unit(0)
+            tables_half(0, 1)
+            for t in range(1, NT):
+                x_tile(t)
+        mx_unit(0)
+        for k in range(1, NU + 1):
+            if k < NU:
+                w_unit(k)
+                tables_half((k + 1) // 2, (k + 1) % 2)
+            if k > 1:
+                mx_unit(k - 1)

@@ -22,13 +22,12 @@ FLOPS = 2 * S * D * D
 NT = S // P
 NG = D // 512
 NU = 8
+KH = D // 2
 TWO_PI = 2.0 * math.pi
 THR = (496, 576)
 CHUNKS = (3, 2, 1, 0)
-X_EVAC = ("s", "s")
-HEAD = 0
-W_EVAC_V = 2
-LAST_ON_VECTOR = 2
+PERM_H = ()
+TURNS_AT = {1: (2, 3), 3: (0, 1)}
 
 
 def tile_ropeattention_pa_kernel(tc, x, w, out):
@@ -38,19 +37,24 @@ def tile_ropeattention_pa_kernel(tc, x, w, out):
         big = ctx.enter_context(tc.tile_pool(name="big", bufs=1))
         grp = ctx.enter_context(tc.tile_pool(name="grp", bufs=5))
         codes = ctx.enter_context(tc.tile_pool(name="codes", bufs=3))
+        perm = ctx.enter_context(tc.tile_pool(name="perm", bufs=3))
         work = ctx.enter_context(tc.tile_pool(name="work", bufs=3))
         psum = ctx.enter_context(tc.psum_pool(name="psum", bufs=4))
+        ctx.enter_context(tc.manual_schedule())
 
-        x_sb = [big.tile([P, D], BF16, name="x_sb%d" % t) for t in range(NT)]
-        w_sb = [big.tile([P, 2 * D], BF16, name="w_sb%d" % k) for k in range(NU)]
+        x_sb = [[big.tile([P, KH], BF16, name="x_sb%d_%d" % (t, h)) for h in range(2)] for t in range(NT)]
+        w_sb = [[big.tile([P, 2 * KH], BF16, name="w_sb%d_%d" % (k, h)) for h in range(2)] for k in range(NU)]
 
         def load_x(t):
-            nc.sync.dma_start(out=x_sb[t][:], in_=x[t * P:(t + 1) * P, :])
+            for h in range(2):
+                nc.sync.dma_start(out=x_sb[t][h][:], in_=x[t * P:(t + 1) * P, h * KH:(h + 1) * KH])
 
         def load_w(k):
             n, e = CHUNKS[k // 2], k % 2
             rows = w[n * 512:(n + 1) * 512, :].rearrange("(a p e) k -> e p a k", a=2, e=2)
-            nc.sync.dma_start(out=w_sb[k][:].rearrange("p (a k) -> p a k", a=2), in_=rows[e])
+            for h in range(2):
+                nc.sync.dma_start(out=w_sb[k][h][:].rearrange("p (a k) -> p a k", a=2),
+                                  in_=rows[e][:, :, h * KH:(h + 1) * KH])
 
         load_x(0)
         load_w(0)
@@ -62,20 +66,15 @@ def tile_ropeattention_pa_kernel(tc, x, w, out):
         warm = const.tile([P, 2], F32, name="warm")
         nc.vector.memset(warm[:, 0:1], 0.0)
         nc.scalar.activation(out=warm[:, 1:2], in_=warm[:, 0:1], func=ACT.Sin)
-        ident = const.tile([P, P], F32, name="ident")
-        make_identity(nc, ident[:])
         s_int = const.tile([P, NT], I32, name="s_int")
         nc.gpsimd.iota(s_int[:], pattern=[[P, NT]], base=0, channel_multiplier=1)
+        ident = const.tile([P, P], F32, name="ident")
+        make_identity(nc, ident[:])
         sc = const.tile([P, 16], F32, name="sc")
-        nc.vector.tensor_copy(out=sc[:, 0:4], in_=s_int[:])
-        nc.vector.tensor_scalar(out=sc[:, 4:8], in0=sc[:, 0:4], scalar1=-1.0, scalar2=None, op0=ALU.mult)
-        nc.vector.tensor_scalar(out=sc[:, 8:12], in0=sc[:, 0:4], scalar1=1.0 / TWO_PI, scalar2=None, op0=ALU.mult)
-        nc.vector.memset(sc[:, 12:13], 1.0)
-        nc.vector.tensor_scalar(out=sc[:, 13:14], in0=sc[:, 12:13], scalar1=0.5 * math.pi, scalar2=None, op0=ALU.mult)
-        half_pi = sc[:, 13:14]
-
         freq = const.tile([P, HALF], F32, name="freq")
         nc.vector.memset(freq[:, 0:1], 1.0)
+        nc.vector.memset(sc[:, 12:13], 1.0)
+        nc.vector.tensor_copy(out=sc[:, 0:4], in_=s_int[:])
         size = 1
         while size < HALF:
             for m in range(1, 4):
@@ -84,6 +83,10 @@ def tile_ropeattention_pa_kernel(tc, x, w, out):
                     scalar1=BASE ** (-(m * size) / HALF), scalar2=None, op0=ALU.mult,
                 )
             size *= 4
+        nc.vector.tensor_scalar(out=sc[:, 4:8], in0=sc[:, 0:4], scalar1=-1.0, scalar2=None, op0=ALU.mult)
+        nc.vector.tensor_scalar(out=sc[:, 13:14], in0=sc[:, 12:13], scalar1=0.5 * math.pi, scalar2=None, op0=ALU.mult)
+        nc.vector.tensor_scalar(out=sc[:, 8:12], in0=sc[:, 0:4], scalar1=1.0 / TWO_PI, scalar2=None, op0=ALU.mult)
+        half_pi = sc[:, 13:14]
 
         frac = [const.tile([P, 2, THR[tp]], F32, name="frac%d" % tp) for tp in range(2)]
         afr = [const.tile([P, 2, THR[tp]], F32, name="afr%d" % tp) for tp in range(2)]
@@ -121,108 +124,178 @@ def tile_ropeattention_pa_kernel(tc, x, w, out):
         x_codes = [big.tile([P, 512], U32, name="x_codes%d" % t, align_bytes=64) for t in range(NT)]
         x_scale = [big.tile([P, 512], U8, name="x_scale%d" % t, align_bytes=64) for t in range(NT)]
 
-        def x_tile(t):
-            xw = x_sb[t][:].bitcast(F32)
-            g4 = grp.tile([P, 2048], BF16, name="g4", align_bytes=64)
-            g4w = g4[:].bitcast(F32)
-            for b in range(2):
-                bank = psum.tile([P, 512], F32, name="tp")
-                for gl in range(2):
-                    for u in range(2):
-                        g = 2 * b + gl
-                        nc.tensor.transpose(bank[:, (2 * gl + u) * P:(2 * gl + u + 1) * P],
-                                            xw[:, g * 2 * P + u:(g + 1) * 2 * P:2], ident[:])
-                dst = g4w[:, b * 512:(b + 1) * 512].rearrange("p (g r u) -> p g r u", g=2, u=2)
-                src = bank[:].rearrange("p (g u r) -> p g r u", g=2, u=2)
-                if X_EVAC[b] == "v":
-                    nc.vector.tensor_copy(out=dst, in_=src)
-                else:
-                    nc.scalar.copy(out=dst, in_=src)
-            nc.vector.quantize_mx(out=x_codes[t][:].bitcast(FP8X4), scales=x_scale[t][:], in_=g4[:])
+        def copy_out(eng, dst, src):
+            if eng == "v":
+                nc.vector.tensor_copy(out=dst, in_=src)
+            else:
+                nc.scalar.copy(out=dst, in_=src)
+
+        def regroup(raw, n):
+            out_t = perm.tile([P, 2 * KH], BF16, name="perm")
+            nc.vector.tensor_copy(out=out_t[:, 0:n].rearrange("p (u c i) -> p u c i", u=2, i=16),
+                                  in_=raw[:].rearrange("p (c u i) -> p u c i", u=2, i=16))
+            return out_t
+
+        def words_of(raw, n, h):
+            return (regroup(raw, n) if h in PERM_H else raw)[:].bitcast(F32)
+
+        def columns(words, h, a, gl, u, na):
+            if h in PERM_H:
+                c0 = u * na * 256 + a * 256 + gl * P
+                return words[:, c0:c0 + P]
+            c0 = a * 512 + gl * 2 * P
+            return words[:, c0 + u:c0 + 2 * P:2]
+
+        x_g4 = {}
+        pend = {}
+
+        def x_turn(t, h):
+            words = words_of(x_sb[t][h], KH, h)
+            bank = psum.tile([P, 512], F32, name="tp")
+            for gl in range(2):
+                for u in range(2):
+                    nc.tensor.transpose(bank[:, (2 * gl + u) * P:(2 * gl + u + 1) * P],
+                                        columns(words, h, 0, gl, u, 1), ident[:])
+            pend["x", t, h] = bank
+
+        def x_out(t, h, eng):
+            if h == 0:
+                x_g4[t] = grp.tile([P, 2048], BF16, name="g4", align_bytes=64)
+            bank = pend["x", t, h]
+            copy_out(eng, x_g4[t][:].bitcast(F32)[:, h * 512:(h + 1) * 512].rearrange("p (g r u) -> p g r u", g=2, u=2),
+                     bank[:].rearrange("p (g u r) -> p g r u", g=2, u=2))
+
+        def x_quant(t):
+            nc.vector.quantize_mx(out=x_codes[t][:].bitcast(FP8X4), scales=x_scale[t][:], in_=x_g4[t][:])
 
         w_codes = {}
         w_scale = {}
+        w_g4 = {}
 
-        def w_unit(k):
-            ww = w_sb[k][:].bitcast(F32)
-            w_codes[k] = codes.tile([P, 1024], U32, name="w_codes", align_bytes=64)
-            w_scale[k] = codes.tile([P, 1024], U8, name="w_scale", align_bytes=64)
-            for h in range(2):
-                g4 = grp.tile([P, 2048], BF16, name="g4", align_bytes=64)
-                g4w = g4[:].bitcast(F32)
-                for gl in range(2):
-                    g = 2 * h + gl
-                    bank = psum.tile([P, 512], F32, name="tp")
-                    for u in range(2):
-                        for e in range(2):
-                            c0 = e * 1024 + g * 2 * P
-                            nc.tensor.transpose(bank[:, (2 * u + e) * P:(2 * u + e + 1) * P],
-                                                ww[:, c0 + u:c0 + 2 * P:2], ident[:])
-                    dst = g4w[:, gl * 512:(gl + 1) * 512].rearrange("p (c u) -> p c u", u=2)
-                    src = bank[:].rearrange("p (u c) -> p c u", u=2)
-                    if k < W_EVAC_V and gl == 1:
-                        nc.vector.tensor_copy(out=dst, in_=src)
-                    else:
-                        nc.scalar.copy(out=dst, in_=src)
-                nc.vector.quantize_mx(out=w_codes[k][:, h * 512:(h + 1) * 512].bitcast(FP8X4),
-                                      scales=w_scale[k][:, h * 512:(h + 1) * 512], in_=g4[:])
+        def w_turn(k, h):
+            words = words_of(w_sb[k][h], 2 * KH, h)
+            for gl in range(2):
+                bank = psum.tile([P, 512], F32, name="tp")
+                for u in range(2):
+                    for a in range(2):
+                        nc.tensor.transpose(bank[:, (2 * u + a) * P:(2 * u + a + 1) * P],
+                                            columns(words, h, a, gl, u, 2), ident[:])
+                pend[k, h, gl] = bank
 
-        first_products = {}
+        def w_out(k, h, engs):
+            g4 = grp.tile([P, 2048], BF16, name="g4", align_bytes=64)
+            w_g4[k, h] = g4
+            g4w = g4[:].bitcast(F32)
+            for gl in range(2):
+                copy_out(engs[gl], g4w[:, gl * 512:(gl + 1) * 512].rearrange("p (c u) -> p c u", u=2),
+                         pend[k, h, gl][:].rearrange("p (u c) -> p c u", u=2))
 
-        def mx_unit(k):
+        def w_quant(k, h):
+            if h == 0:
+                w_codes[k] = codes.tile([P, 1024], U32, name="w_codes", align_bytes=64)
+                w_scale[k] = codes.tile([P, 1024], U8, name="w_scale", align_bytes=64)
+            nc.vector.quantize_mx(out=w_codes[k][:, h * 512:(h + 1) * 512].bitcast(FP8X4),
+                                  scales=w_scale[k][:, h * 512:(h + 1) * 512], in_=w_g4[k, h][:])
+
+        prods = {}
+        banks = {}
+
+        def multiply(k, tiles):
+            y = psum.tile([P, 512], F32, name="tp" if k == NU - 1 else "y")
+            for j, t in enumerate(tiles):
+                for g in range(NG):
+                    nc.tensor.matmul_mx(
+                        out=y[:, j * 256:(j + 1) * 256],
+                        lhsT=x_codes[t][:, g * P:(g + 1) * P].bitcast(FP8X4),
+                        lhsT_scale=x_scale[t][:, g * P:(g + 1) * P],
+                        rhs=w_codes[k][:, g * 256:(g + 1) * 256].bitcast(FP8X4),
+                        rhs_scale=w_scale[k][:, g * 256:(g + 1) * 256],
+                        start=(g == 0), stop=(g == NG - 1),
+                    )
+            banks[k, tiles[0]] = y
+
+        def products(k, tiles):
             n, e = CHUNKS[k // 2], k % 2
-            last = k == NU - 1
-            groups = [(t,) for t in range(NT)] if last else [(0, 1), (2, 3)]
-            for tiles in groups:
-                nt = len(tiles)
-                y = psum.tile([P, 512], F32, name="tp" if last else "y")
-                for j, t in enumerate(tiles):
-                    for g in range(NG):
-                        nc.tensor.matmul_mx(
-                            out=y[:, j * 256:(j + 1) * 256],
-                            lhsT=x_codes[t][:, g * P:(g + 1) * P].bitcast(FP8X4),
-                            lhsT_scale=x_scale[t][:, g * P:(g + 1) * P],
-                            rhs=w_codes[k][:, g * 256:(g + 1) * 256].bitcast(FP8X4),
-                            rhs_scale=w_scale[k][:, g * 256:(g + 1) * 256],
-                            start=(g == 0), stop=(g == NG - 1),
-                        )
-                prod = work.tile([P, 2, 256, 2], F32, name="pa" if e == 0 else "pb", bufs=4 if e == 0 else 3)
-                nc.vector.tensor_tensor(
-                    out=prod[:, 0:nt],
-                    in0=y[:, 0:nt * 256].rearrange("p (t r) -> p t r", t=nt).unsqueeze(3).to_broadcast([P, nt, 256, 2]),
-                    in1=tab[n][:, tiles[0]:tiles[0] + nt, 1 - e:3 - e, :].rearrange("p t c r -> p t r c"),
-                    op=ALU.mult,
-                )
-                if e == 0:
-                    first_products[tiles[0] // 2] = prod
-                else:
-                    eng = nc.vector if (last and tiles[0] >= LAST_ON_VECTOR) else nc.gpsimd
-                    for j, t in enumerate(tiles):
-                        res = first_products[t // 2][:, t % 2]
-                        eng.tensor_tensor(out=res, in0=res, in1=prod[:, j], op=ALU.add)
-                        nc.sync.dma_start(out=out[t * P:(t + 1) * P, n * 512:(n + 1) * 512],
-                                          in_=res.rearrange("p r c -> p (r c)"))
+            nt, j0 = len(tiles), tiles[0] % 2
+            if j0 == 0:
+                prods[k, tiles[0] // 2] = work.tile([P, 2, 256, 2], F32, name="pa" if e == 0 else "pb",
+                                                    bufs=4 if e == 0 else 3)
+            prod = prods[k, tiles[0] // 2]
+            y = banks[k, tiles[0]]
+            nc.vector.tensor_tensor(
+                out=prod[:, j0:j0 + nt],
+                in0=y[:, 0:nt * 256].rearrange("p (t r) -> p t r", t=nt).unsqueeze(3).to_broadcast([P, nt, 256, 2]),
+                in1=tab[n][:, tiles[0]:tiles[0] + nt, 1 - e:3 - e, :].rearrange("p t c r -> p t r c"),
+                op=ALU.mult,
+            )
 
+        def add_store(k, tiles, eng):
+            n = CHUNKS[k // 2]
+            for t in tiles:
+                res = prods[k - 1, t // 2][:, t % 2]
+                (nc.vector if eng == "v" else nc.gpsimd).tensor_tensor(out=res, in0=res, in1=prods[k, t // 2][:, t % 2],
+                                                                      op=ALU.add)
+                nc.sync.dma_start(out=out[t * P:(t + 1) * P, n * 512:(n + 1) * 512],
+                                  in_=res.rearrange("p r c -> p (r c)"))
+
+        PAIRS = ((0, 1), (2, 3))
+        x_turn(0, 0)
+        x_turn(0, 1)
+        tables_half(0, 0)
+        x_out(0, 0, "s")
+        x_out(0, 1, "v")
+        w_turn(0, 0)
+        w_out(0, 0, "sv")
+        x_quant(0)
+        w_turn(0, 1)
+        w_out(0, 1, "sv")
+        w_quant(0, 0)
+        x_turn(1, 0)
+        x_turn(1, 1)
+        x_out(1, 0, "s")
+        x_out(1, 1, "v")
+        w_quant(0, 1)
+        x_turn(2, 0)
+        x_turn(2, 1)
+        x_out(2, 0, "s")
+        x_out(2, 1, "v")
+        x_quant(1)
+        x_turn(3, 0)
+        x_turn(3, 1)
+        x_out(3, 0, "s")
+        x_out(3, 1, "v")
+        x_quant(2)
+        x_quant(3)
+        tables_half(0, 1)
+        for k in range(1, NU):
+            w_turn(k, 0)
+            w_out(k, 0, "ss")
+            if k >= 2:
+                products(k - 2, PAIRS[1])
+                if k % 2 == 1:
+                    add_store(k - 2, PAIRS[1], "g")
+            w_turn(k, 1)
+            w_out(k, 1, "ss")
+            w_quant(k, 0)
+            w_quant(k, 1)
+            for t in TURNS_AT.get(k, ()):
+                reduce_turns(t)
+            tables_half((k + 1) // 2, (k + 1) % 2)
+            if k < NU - 1:
+                multiply(k - 1, PAIRS[0])
+                products(k - 1, PAIRS[0])
+                if k % 2 == 0:
+                    add_store(k - 1, PAIRS[0], "g")
+                multiply(k - 1, PAIRS[1])
+        k = NU - 2
         for t in range(NT):
-            reduce_turns(t)
-        if HEAD == 0:
-            x_tile(0)
-            w_unit(0)
-            for t in range(1, NT):
-                x_tile(t)
-            tables_half(0, 0)
-            tables_half(0, 1)
-        elif HEAD == 1:
-            tables_half(0, 0)
-            x_tile(0)
-            w_unit(0)
-            tables_half(0, 1)
-            for t in range(1, NT):
-                x_tile(t)
-        mx_unit(0)
-        for k in range(1, NU + 1):
-            if k < NU:
-                w_unit(k)
-                tables_half((k + 1) // 2, (k + 1) % 2)
-            if k > 1:
-                mx_unit(k - 1)
+            multiply(k, (t,))
+            products(k, (t,))
+        k = NU - 1
+        for t in range(NT):
+            multiply(k, (t,))
+            products(k, (t,))
+            if t < 2:
+                add_store(k, (t,), "g")
+        add_store(k, (2,), "v")
+        add_store(k, (3,), "v")

@@ -23,11 +23,12 @@ NT = S // P
 NG = D // 512
 NU = 8
 KH = D // 2
+H_ORDER = (0, 1)
 TWO_PI = 2.0 * math.pi
 THR = (496, 576)
 CHUNKS = (3, 2, 1, 0)
 PERM_H = ()
-TURNS_AT = {1: (2, 3), 3: (0, 1)}
+TURNS_AT = {1: (2, 3), 2: (0, 1)}
 
 
 def tile_ropeattention_pa_kernel(tc, x, w, out):
@@ -46,13 +47,13 @@ def tile_ropeattention_pa_kernel(tc, x, w, out):
         w_sb = [[big.tile([P, 2 * KH], BF16, name="w_sb%d_%d" % (k, h)) for h in range(2)] for k in range(NU)]
 
         def load_x(t):
-            for h in range(2):
+            for h in H_ORDER:
                 nc.sync.dma_start(out=x_sb[t][h][:], in_=x[t * P:(t + 1) * P, h * KH:(h + 1) * KH])
 
         def load_w(k):
             n, e = CHUNKS[k // 2], k % 2
             rows = w[n * 512:(n + 1) * 512, :].rearrange("(a p e) k -> e p a k", a=2, e=2)
-            for h in range(2):
+            for h in H_ORDER:
                 nc.sync.dma_start(out=w_sb[k][h][:].rearrange("p (a k) -> p a k", a=2),
                                   in_=rows[e][:, :, h * KH:(h + 1) * KH])
 
@@ -100,26 +101,36 @@ def tile_ropeattention_pa_kernel(tc, x, w, out):
                                            in1=turns[:, 0:hi].bitcast(I32), op0=ALU.mult, op1=ALU.subtract)
 
         def tables_half(c, tp):
+            calls = []
             if c >= len(CHUNKS):
-                return
+                return calls
             n = CHUNKS[c]
             lo, hi = 256 * n, 256 * (n + 1)
             mid = min(max(THR[tp], lo), hi)
             both = slice(2 * tp, 2 * tp + 2)
             if mid > lo:
-                nc.scalar.activation(out=afr[tp][:, :, lo:mid], in_=frac[tp][:, :, lo:mid], func=ACT.Abs)
-                nc.scalar.activation(out=tab[n][:, both, 2, 0:mid - lo], in_=frac[tp][:, :, lo:mid], func=ACT.Sin,
-                                     scale=TWO_PI)
-                nc.scalar.activation(out=tab[n][:, both, 1, 0:mid - lo], in_=afr[tp][:, :, lo:mid], func=ACT.Sin,
-                                     scale=-TWO_PI, bias=half_pi)
+                calls.append(lambda: nc.scalar.activation(
+                    out=afr[tp][:, :, lo:mid], in_=frac[tp][:, :, lo:mid], func=ACT.Abs))
+                calls.append(lambda: nc.scalar.activation(
+                    out=tab[n][:, both, 2, 0:mid - lo], in_=frac[tp][:, :, lo:mid], func=ACT.Sin, scale=TWO_PI))
+                calls.append(lambda: nc.scalar.activation(
+                    out=tab[n][:, both, 1, 0:mid - lo], in_=afr[tp][:, :, lo:mid], func=ACT.Sin,
+                    scale=-TWO_PI, bias=half_pi))
             if mid < hi:
                 for t in (2 * tp, 2 * tp + 1):
-                    nc.scalar.activation(out=tab[n][:, t, 2, mid - lo:256], in_=freq[:, mid:hi], func=ACT.Sin,
-                                         scale=sc[:, t:t + 1])
-                    nc.scalar.activation(out=tab[n][:, t, 1, mid - lo:256], in_=freq[:, mid:hi], func=ACT.Sin,
-                                         scale=sc[:, 4 + t:5 + t], bias=half_pi)
-            nc.gpsimd.tensor_scalar(out=tab[n][:, both, 0, :], in0=tab[n][:, both, 2, :],
-                                    scalar1=-1.0, scalar2=0.0, op0=ALU.mult, op1=ALU.add)
+                    calls.append(lambda t=t: nc.scalar.activation(
+                        out=tab[n][:, t, 2, mid - lo:256], in_=freq[:, mid:hi], func=ACT.Sin, scale=sc[:, t:t + 1]))
+                    calls.append(lambda t=t: nc.scalar.activation(
+                        out=tab[n][:, t, 1, mid - lo:256], in_=freq[:, mid:hi], func=ACT.Sin,
+                        scale=sc[:, 4 + t:5 + t], bias=half_pi))
+            calls.append(lambda: nc.gpsimd.tensor_scalar(
+                out=tab[n][:, both, 0, :], in0=tab[n][:, both, 2, :],
+                scalar1=-1.0, scalar2=0.0, op0=ALU.mult, op1=ALU.add))
+            return calls
+
+        def run(calls):
+            for call in calls:
+                call()
 
         x_codes = [big.tile([P, 512], U32, name="x_codes%d" % t, align_bytes=64) for t in range(NT)]
         x_scale = [big.tile([P, 512], U8, name="x_scale%d" % t, align_bytes=64) for t in range(NT)]
@@ -136,8 +147,11 @@ def tile_ropeattention_pa_kernel(tc, x, w, out):
                                   in_=raw[:].rearrange("p (c u i) -> p u c i", u=2, i=16))
             return out_t
 
-        def words_of(raw, n, h):
-            return (regroup(raw, n) if h in PERM_H else raw)[:].bitcast(F32)
+        ready = {}
+
+        def prepare(key, raw, n):
+            for h in H_ORDER:
+                ready[key, h] = (regroup(raw[h], n) if h in PERM_H else raw[h])[:].bitcast(F32)
 
         def columns(words, h, a, gl, u, na):
             if h in PERM_H:
@@ -150,7 +164,7 @@ def tile_ropeattention_pa_kernel(tc, x, w, out):
         pend = {}
 
         def x_turn(t, h):
-            words = words_of(x_sb[t][h], KH, h)
+            words = ready[("x", t), h]
             bank = psum.tile([P, 512], F32, name="tp")
             for gl in range(2):
                 for u in range(2):
@@ -159,7 +173,7 @@ def tile_ropeattention_pa_kernel(tc, x, w, out):
             pend["x", t, h] = bank
 
         def x_out(t, h, eng):
-            if h == 0:
+            if t not in x_g4:
                 x_g4[t] = grp.tile([P, 2048], BF16, name="g4", align_bytes=64)
             bank = pend["x", t, h]
             copy_out(eng, x_g4[t][:].bitcast(F32)[:, h * 512:(h + 1) * 512].rearrange("p (g r u) -> p g r u", g=2, u=2),
@@ -173,7 +187,7 @@ def tile_ropeattention_pa_kernel(tc, x, w, out):
         w_g4 = {}
 
         def w_turn(k, h):
-            words = words_of(w_sb[k][h], 2 * KH, h)
+            words = ready[("w", k), h]
             for gl in range(2):
                 bank = psum.tile([P, 512], F32, name="tp")
                 for u in range(2):
@@ -191,7 +205,7 @@ def tile_ropeattention_pa_kernel(tc, x, w, out):
                          pend[k, h, gl][:].rearrange("p (u c) -> p c u", u=2))
 
         def w_quant(k, h):
-            if h == 0:
+            if k not in w_codes:
                 w_codes[k] = codes.tile([P, 1024], U32, name="w_codes", align_bytes=64)
                 w_scale[k] = codes.tile([P, 1024], U8, name="w_scale", align_bytes=64)
             nc.vector.quantize_mx(out=w_codes[k][:, h * 512:(h + 1) * 512].bitcast(FP8X4),
@@ -239,63 +253,78 @@ def tile_ropeattention_pa_kernel(tc, x, w, out):
                                   in_=res.rearrange("p r c -> p (r c)"))
 
         PAIRS = ((0, 1), (2, 3))
-        x_turn(0, 0)
-        x_turn(0, 1)
-        tables_half(0, 0)
-        x_out(0, 0, "s")
-        x_out(0, 1, "v")
-        w_turn(0, 0)
-        w_out(0, 0, "sv")
+        HA, HB = H_ORDER
+        prepare(("x", 0), x_sb[0], KH)
+        x_turn(0, HA)
+        x_turn(0, HB)
+        run(tables_half(0, 0))
+        x_out(0, HA, "s")
+        x_out(0, HB, "v")
+        prepare(("w", 0), w_sb[0], 2 * KH)
+        w_turn(0, HA)
+        w_out(0, HA, "sv")
         x_quant(0)
-        w_turn(0, 1)
-        w_out(0, 1, "sv")
-        w_quant(0, 0)
-        x_turn(1, 0)
-        x_turn(1, 1)
-        x_out(1, 0, "s")
-        x_out(1, 1, "v")
-        w_quant(0, 1)
-        x_turn(2, 0)
-        x_turn(2, 1)
-        x_out(2, 0, "s")
-        x_out(2, 1, "v")
+        w_turn(0, HB)
+        prepare(("x", 1), x_sb[1], KH)
+        w_out(0, HB, "sv")
+        w_quant(0, HA)
+        x_turn(1, HA)
+        x_turn(1, HB)
+        prepare(("x", 2), x_sb[2], KH)
+        x_out(1, HA, "s")
+        x_out(1, HB, "v")
+        w_quant(0, HB)
+        x_turn(2, HA)
+        x_turn(2, HB)
+        prepare(("x", 3), x_sb[3], KH)
+        x_out(2, HA, "s")
+        x_out(2, HB, "v")
         x_quant(1)
-        x_turn(3, 0)
-        x_turn(3, 1)
-        x_out(3, 0, "s")
-        x_out(3, 1, "v")
+        x_turn(3, HA)
+        x_turn(3, HB)
+        prepare(("w", 1), w_sb[1], 2 * KH)
+        x_out(3, HA, "s")
+        x_out(3, HB, "v")
         x_quant(2)
         x_quant(3)
-        tables_half(0, 1)
+        run(tables_half(0, 1))
+        turned = []
+        multiplied = []
+        waiting = [(0, PAIRS[0]), (0, PAIRS[1])]
+
+        def vector_step():
+            while turned:
+                w_quant(*turned.pop(0))
+            while multiplied:
+                k0, tiles = multiplied.pop(0)
+                products(k0, tiles)
+                if k0 % 2 == 1:
+                    add_store(k0, tiles, "g")
+
         for k in range(1, NU):
-            w_turn(k, 0)
-            w_out(k, 0, "ss")
-            if k >= 2:
-                products(k - 2, PAIRS[1])
-                if k % 2 == 1:
-                    add_store(k - 2, PAIRS[1], "g")
-            w_turn(k, 1)
-            w_out(k, 1, "ss")
-            w_quant(k, 0)
-            w_quant(k, 1)
-            for t in TURNS_AT.get(k, ()):
-                reduce_turns(t)
-            tables_half((k + 1) // 2, (k + 1) % 2)
-            if k < NU - 1:
-                multiply(k - 1, PAIRS[0])
-                products(k - 1, PAIRS[0])
-                if k % 2 == 0:
-                    add_store(k - 1, PAIRS[0], "g")
-                multiply(k - 1, PAIRS[1])
-        k = NU - 2
-        for t in range(NT):
-            multiply(k, (t,))
-            products(k, (t,))
-        k = NU - 1
-        for t in range(NT):
-            multiply(k, (t,))
-            products(k, (t,))
-            if t < 2:
-                add_store(k, (t,), "g")
-        add_store(k, (2,), "v")
-        add_store(k, (3,), "v")
+            calls = tables_half((k + 1) // 2, (k + 1) % 2)
+            cut = len(calls) // 2
+            for i, h in enumerate(H_ORDER):
+                w_turn(k, h)
+                w_out(k, h, "ss")
+                vector_step()
+                turned.append((k, h))
+                if i == 0:
+                    if k + 1 < NU:
+                        prepare(("w", k + 1), w_sb[k + 1], 2 * KH)
+                    for t in TURNS_AT.get(k, ()):
+                        reduce_turns(t)
+                    run(calls[:cut])
+                else:
+                    run(calls[cut:])
+                if (k, i) != (1, 0):
+                    k0, tiles = waiting.pop(0)
+                    multiply(k0, tiles)
+                    multiplied.append((k0, tiles))
+            waiting += [(k, (t,)) for t in range(NT)] if k >= NU - 1 else [(k, PAIRS[0]), (k, PAIRS[1])]
+        vector_step()
+        for k0, tiles in waiting:
+            multiply(k0, tiles)
+            products(k0, tiles)
+            if k0 % 2 == 1:
+                add_store(k0, tiles, "g" if tiles[0] < 2 else "v")

@@ -64,6 +64,15 @@ def tile_ropeattention_pa_kernel(tc, x, w, out):
         for k in range(1, NU):
             load_w(k)
 
+        zeros = const.tile([P, 512], BF16, name="zeros")
+        nc.vector.memset(zeros[:], 0.0)
+
+        def keep_clock(n):
+            idle = psum.tile([P, 512], F32, name="y")
+            for i in range(n):
+                nc.tensor.matmul(idle[:], lhsT=zeros[:, 0:P], rhs=zeros[:], start=True, stop=True)
+
+        keep_clock(5)
         warm = const.tile([P, 2], F32, name="warm")
         nc.vector.memset(warm[:, 0:1], 0.0)
         nc.scalar.activation(out=warm[:, 1:2], in_=warm[:, 0:1], func=ACT.Sin)
@@ -257,6 +266,7 @@ def tile_ropeattention_pa_kernel(tc, x, w, out):
         prepare(("x", 0), x_sb[0], KH)
         x_turn(0, HA)
         x_turn(0, HB)
+        keep_clock(2)
         run(tables_half(0, 0))
         x_out(0, HA, "s")
         x_out(0, HB, "v")
@@ -264,24 +274,29 @@ def tile_ropeattention_pa_kernel(tc, x, w, out):
         w_turn(0, HA)
         w_out(0, HA, "sv")
         x_quant(0)
+        keep_clock(2)
         w_turn(0, HB)
+        keep_clock(2)
         prepare(("x", 1), x_sb[1], KH)
         w_out(0, HB, "sv")
         w_quant(0, HA)
         x_turn(1, HA)
         x_turn(1, HB)
+        keep_clock(2)
         prepare(("x", 2), x_sb[2], KH)
         x_out(1, HA, "s")
         x_out(1, HB, "v")
         w_quant(0, HB)
         x_turn(2, HA)
         x_turn(2, HB)
+        keep_clock(2)
         prepare(("x", 3), x_sb[3], KH)
         x_out(2, HA, "s")
         x_out(2, HB, "v")
         x_quant(1)
         x_turn(3, HA)
         x_turn(3, HB)
+        keep_clock(2)
         prepare(("w", 1), w_sb[1], 2 * KH)
         x_out(3, HA, "s")
         x_out(3, HB, "v")
@@ -317,7 +332,9 @@ def tile_ropeattention_pa_kernel(tc, x, w, out):
                     run(calls[:cut])
                 else:
                     run(calls[cut:])
-                if (k, i) != (1, 0):
+                if (k, i) == (1, 0):
+                    keep_clock(2)
+                else:
                     k0, tiles = waiting.pop(0)
                     multiply(k0, tiles)
                     multiplied.append((k0, tiles))

@@ -29,6 +29,7 @@ THR = (496, 576)
 CHUNKS = (3, 2, 1, 0)
 PERM_H = ()
 TURNS_AT = {1: (2, 3), 2: (0, 1)}
+OPT = {"turn_eng": 's', "turn_head": ((2, 's'), (3, 's')), "turn_lag": 1, "neg": 'v', "xout": 'sv', "perm": {(('x', 2), 0): 'v', (('x', 2), 1): 'v'}, "add": 'gggg', "addlast": 'gvgv', "d0": 4, "d1": 2, "d2": 1, "d3": 2, "d4": 2, "d5": 0, "m0": (1,), "mc": (1, 1, 1, 2, 2, 2, 2, 2, 2, 2, 2, 2, 2, 2), "addk": {}, "qfirst": True, "w0out": 'ss', "tabhead": 1, "wouts": 'ss', "rq": 0, "pb": 4, "single": 7}
 
 
 def tile_ropeattention_pa_kernel(tc, x, w, out):
@@ -38,7 +39,7 @@ def tile_ropeattention_pa_kernel(tc, x, w, out):
         big = ctx.enter_context(tc.tile_pool(name="big", bufs=1))
         grp = ctx.enter_context(tc.tile_pool(name="grp", bufs=5))
         codes = ctx.enter_context(tc.tile_pool(name="codes", bufs=3))
-        perm = ctx.enter_context(tc.tile_pool(name="perm", bufs=3))
+        perm = ctx.enter_context(tc.tile_pool(name="perm", bufs=2))
         work = ctx.enter_context(tc.tile_pool(name="work", bufs=3))
         psum = ctx.enter_context(tc.psum_pool(name="psum", bufs=4))
         ctx.enter_context(tc.manual_schedule())
@@ -51,11 +52,11 @@ def tile_ropeattention_pa_kernel(tc, x, w, out):
                 nc.sync.dma_start(out=x_sb[t][h][:], in_=x[t * P:(t + 1) * P, h * KH:(h + 1) * KH])
 
         def load_w(k):
-            n, e = CHUNKS[k // 2], k % 2
-            rows = w[n * 512:(n + 1) * 512, :].rearrange("(a p e) k -> e p a k", a=2, e=2)
+            c0 = CHUNKS[k // 2] * 512 + k % 2 * 256
+            rows = w[c0:c0 + 256, :].rearrange("(p e) k -> p e k", e=2)
             for h in H_ORDER:
-                nc.sync.dma_start(out=w_sb[k][h][:].rearrange("p (a k) -> p a k", a=2),
-                                  in_=rows[e][:, :, h * KH:(h + 1) * KH])
+                nc.sync.dma_start(out=w_sb[k][h][:].rearrange("p (e k) -> p e k", e=2),
+                                  in_=rows[:, :, h * KH:(h + 1) * KH])
 
         load_x(0)
         load_w(0)
@@ -65,14 +66,14 @@ def tile_ropeattention_pa_kernel(tc, x, w, out):
             load_w(k)
 
         zeros = const.tile([P, 512], BF16, name="zeros")
-        nc.vector.memset(zeros[:], 0.0)
+        nc.vector.memset(zeros[:].bitcast(I32), 0)
 
         def keep_clock(n):
             idle = psum.tile([P, 512], F32, name="y")
             for i in range(n):
                 nc.tensor.matmul(idle[:], lhsT=zeros[:, 0:P], rhs=zeros[:], start=True, stop=True)
 
-        keep_clock(5)
+        keep_clock(OPT["d0"])
         warm = const.tile([P, 2], F32, name="warm")
         nc.vector.memset(warm[:, 0:1], 0.0)
         nc.scalar.activation(out=warm[:, 1:2], in_=warm[:, 0:1], func=ACT.Sin)
@@ -85,6 +86,7 @@ def tile_ropeattention_pa_kernel(tc, x, w, out):
         nc.vector.memset(freq[:, 0:1], 1.0)
         nc.vector.memset(sc[:, 12:13], 1.0)
         nc.vector.tensor_copy(out=sc[:, 0:4], in_=s_int[:])
+        nc.vector.tensor_scalar(out=sc[:, 8:12], in0=sc[:, 0:4], scalar1=1.0 / TWO_PI, scalar2=None, op0=ALU.mult)
         size = 1
         while size < HALF:
             for m in range(1, 4):
@@ -95,19 +97,28 @@ def tile_ropeattention_pa_kernel(tc, x, w, out):
             size *= 4
         nc.vector.tensor_scalar(out=sc[:, 4:8], in0=sc[:, 0:4], scalar1=-1.0, scalar2=None, op0=ALU.mult)
         nc.vector.tensor_scalar(out=sc[:, 13:14], in0=sc[:, 12:13], scalar1=0.5 * math.pi, scalar2=None, op0=ALU.mult)
-        nc.vector.tensor_scalar(out=sc[:, 8:12], in0=sc[:, 0:4], scalar1=1.0 / TWO_PI, scalar2=None, op0=ALU.mult)
         half_pi = sc[:, 13:14]
 
         frac = [const.tile([P, 2, THR[tp]], F32, name="frac%d" % tp) for tp in range(2)]
         afr = [const.tile([P, 2, THR[tp]], F32, name="afr%d" % tp) for tp in range(2)]
         tab = [const.tile([P, NT, 3, 256], F32, name="tab%d" % n) for n in range(4)]
 
-        def reduce_turns(t):
+        turns_of = {}
+
+        def count_turns(t, eng):
             hi = THR[t // 2]
-            turns = work.tile([P, 576], U32, name="turns", bufs=2)
-            nc.scalar.activation(out=turns[:, 0:hi], in_=freq[:, 0:hi], func=ACT.Copy, scale=sc[:, 8 + t:9 + t])
+            turns_of[t] = work.tile([P, 576], I32, name="turns", bufs=2)
+            if eng == "g":
+                nc.gpsimd.tensor_scalar(out=turns_of[t][:, 0:hi], in0=freq[:, 0:hi], scalar1=sc[:, 8 + t:9 + t],
+                                        scalar2=0.0, op0=ALU.mult, op1=ALU.add)
+            else:
+                nc.scalar.activation(out=turns_of[t][:, 0:hi].bitcast(U32), in_=freq[:, 0:hi], func=ACT.Copy,
+                                     scale=sc[:, 8 + t:9 + t])
+
+        def take_turns(t):
+            hi = THR[t // 2]
             nc.vector.scalar_tensor_tensor(out=frac[t // 2][:, t % 2, :], in0=freq[:, 0:hi], scalar=sc[:, 8 + t:9 + t],
-                                           in1=turns[:, 0:hi].bitcast(I32), op0=ALU.mult, op1=ALU.subtract)
+                                           in1=turns_of[t][:, 0:hi], op0=ALU.mult, op1=ALU.subtract)
 
         def tables_half(c, tp):
             calls = []
@@ -132,9 +143,21 @@ def tile_ropeattention_pa_kernel(tc, x, w, out):
                     calls.append(lambda t=t: nc.scalar.activation(
                         out=tab[n][:, t, 1, mid - lo:256], in_=freq[:, mid:hi], func=ACT.Sin,
                         scale=sc[:, 4 + t:5 + t], bias=half_pi))
-            calls.append(lambda: nc.gpsimd.tensor_scalar(
-                out=tab[n][:, both, 0, :], in0=tab[n][:, both, 2, :],
-                scalar1=-1.0, scalar2=0.0, op0=ALU.mult, op1=ALU.add))
+            if OPT["neg"] == "s":
+                if mid > lo:
+                    calls.append(lambda: nc.scalar.activation(
+                        out=tab[n][:, both, 0, 0:mid - lo], in_=frac[tp][:, :, lo:mid], func=ACT.Sin, scale=-TWO_PI))
+                if mid < hi:
+                    for t in (2 * tp, 2 * tp + 1):
+                        calls.append(lambda t=t: nc.scalar.activation(
+                            out=tab[n][:, t, 0, mid - lo:256], in_=freq[:, mid:hi], func=ACT.Sin, scale=sc[:, 4 + t:5 + t]))
+            elif OPT["neg"] == "v":
+                calls.append(lambda: nc.vector.tensor_scalar(
+                    out=tab[n][:, both, 0, :], in0=tab[n][:, both, 2, :], scalar1=-1.0, scalar2=None, op0=ALU.mult))
+            else:
+                calls.append(lambda: nc.gpsimd.tensor_scalar(
+                    out=tab[n][:, both, 0, :], in0=tab[n][:, both, 2, :],
+                    scalar1=-1.0, scalar2=0.0, op0=ALU.mult, op1=ALU.add))
             return calls
 
         def run(calls):
@@ -150,21 +173,24 @@ def tile_ropeattention_pa_kernel(tc, x, w, out):
             else:
                 nc.scalar.copy(out=dst, in_=src)
 
-        def regroup(raw, n):
+        def regroup(raw, na, engs):
             out_t = perm.tile([P, 2 * KH], BF16, name="perm")
-            nc.vector.tensor_copy(out=out_t[:, 0:n].rearrange("p (u c i) -> p u c i", u=2, i=16),
-                                  in_=raw[:].rearrange("p (c u i) -> p u c i", u=2, i=16))
+            src = raw[:].bitcast(F32).rearrange("p (a c u) -> p a u c", a=na, u=2)
+            dst = out_t[:, 0:na * KH].bitcast(F32).rearrange("p (a u c) -> p a u c", a=na, u=2)
+            for a in range(na):
+                copy_out(engs[a], dst[:, a], src[:, a])
             return out_t
 
         ready = {}
 
         def prepare(key, raw, n):
             for h in H_ORDER:
-                ready[key, h] = (regroup(raw[h], n) if h in PERM_H else raw[h])[:].bitcast(F32)
+                engs = OPT["perm"].get((key, h))
+                ready[key, h] = (regroup(raw[h], n // KH, engs) if engs else raw[h])[:].bitcast(F32)
 
-        def columns(words, h, a, gl, u, na):
-            if h in PERM_H:
-                c0 = u * na * 256 + a * 256 + gl * P
+        def columns(words, key, a, gl, u, na):
+            if key in OPT["perm"]:
+                c0 = a * 512 + u * 256 + gl * P
                 return words[:, c0:c0 + P]
             c0 = a * 512 + gl * 2 * P
             return words[:, c0 + u:c0 + 2 * P:2]
@@ -178,7 +204,7 @@ def tile_ropeattention_pa_kernel(tc, x, w, out):
             for gl in range(2):
                 for u in range(2):
                     nc.tensor.transpose(bank[:, (2 * gl + u) * P:(2 * gl + u + 1) * P],
-                                        columns(words, h, 0, gl, u, 1), ident[:])
+                                        columns(words, (("x", t), h), 0, gl, u, 1), ident[:])
             pend["x", t, h] = bank
 
         def x_out(t, h, eng):
@@ -202,7 +228,7 @@ def tile_ropeattention_pa_kernel(tc, x, w, out):
                 for u in range(2):
                     for a in range(2):
                         nc.tensor.transpose(bank[:, (2 * u + a) * P:(2 * u + a + 1) * P],
-                                            columns(words, h, a, gl, u, 2), ident[:])
+                                            columns(words, (("w", k), h), a, gl, u, 2), ident[:])
                 pend[k, h, gl] = bank
 
         def w_out(k, h, engs):
@@ -222,126 +248,158 @@ def tile_ropeattention_pa_kernel(tc, x, w, out):
 
         prods = {}
         banks = {}
+        turned = []
+        multiplied = []
 
-        def multiply(k, tiles):
-            y = psum.tile([P, 512], F32, name="tp" if k == NU - 1 else "y")
-            for j, t in enumerate(tiles):
-                for g in range(NG):
-                    nc.tensor.matmul_mx(
-                        out=y[:, j * 256:(j + 1) * 256],
-                        lhsT=x_codes[t][:, g * P:(g + 1) * P].bitcast(FP8X4),
-                        lhsT_scale=x_scale[t][:, g * P:(g + 1) * P],
-                        rhs=w_codes[k][:, g * 256:(g + 1) * 256].bitcast(FP8X4),
-                        rhs_scale=w_scale[k][:, g * 256:(g + 1) * 256],
-                        start=(g == 0), stop=(g == NG - 1),
-                    )
-            banks[k, tiles[0]] = y
+        def multiply(k, t):
+            j = 0 if k >= OPT["single"] else t % 2
+            if j == 0:
+                banks[k, t] = psum.tile([P, 512], F32, name="tp" if k == NU - 1 else "y")
+            y = banks[k, t - j]
+            for g in range(NG):
+                nc.tensor.matmul_mx(
+                    out=y[:, j * 256:(j + 1) * 256],
+                    lhsT=x_codes[t][:, g * P:(g + 1) * P].bitcast(FP8X4),
+                    lhsT_scale=x_scale[t][:, g * P:(g + 1) * P],
+                    rhs=w_codes[k][:, g * 256:(g + 1) * 256].bitcast(FP8X4),
+                    rhs_scale=w_scale[k][:, g * 256:(g + 1) * 256],
+                    start=(g == 0), stop=(g == NG - 1),
+                )
+            if k >= OPT["single"]:
+                multiplied.append((k, (t,)))
+            elif j == 1:
+                multiplied.append((k, (t - 1, t)))
 
         def products(k, tiles):
-            n, e = CHUNKS[k // 2], k % 2
-            nt, j0 = len(tiles), tiles[0] % 2
-            if j0 == 0:
-                prods[k, tiles[0] // 2] = work.tile([P, 2, 256, 2], F32, name="pa" if e == 0 else "pb",
-                                                    bufs=4 if e == 0 else 3)
-            prod = prods[k, tiles[0] // 2]
+            n, r0 = CHUNKS[k // 2], k % 2 * P
+            nt = len(tiles)
             y = banks[k, tiles[0]]
-            nc.vector.tensor_tensor(
-                out=prod[:, j0:j0 + nt],
-                in0=y[:, 0:nt * 256].rearrange("p (t r) -> p t r", t=nt).unsqueeze(3).to_broadcast([P, nt, 256, 2]),
-                in1=tab[n][:, tiles[0]:tiles[0] + nt, 1 - e:3 - e, :].rearrange("p t c r -> p t r c"),
-                op=ALU.mult,
-            )
+            ye = y[:, 0:nt * 256].rearrange("p (t e r) -> p t e r", t=nt, e=2)
+            prods[k, tiles[0]] = [work.tile([P, nt, P, 2], F32, name="p%d_%d" % (e, nt), bufs=OPT["pb"]) for e in range(2)]
+            for e in range(2):
+                nc.vector.tensor_tensor(
+                    out=prods[k, tiles[0]][e][:],
+                    in0=ye[:, :, e, :].unsqueeze(3).to_broadcast([P, nt, P, 2]),
+                    in1=tab[n][:, tiles[0]:tiles[0] + nt, 1 - e:3 - e, r0:r0 + P].rearrange("p t c r -> p t r c"),
+                    op=ALU.mult,
+                )
 
         def add_store(k, tiles, eng):
-            n = CHUNKS[k // 2]
-            for t in tiles:
-                res = prods[k - 1, t // 2][:, t % 2]
-                (nc.vector if eng == "v" else nc.gpsimd).tensor_tensor(out=res, in0=res, in1=prods[k, t // 2][:, t % 2],
-                                                                      op=ALU.add)
-                nc.sync.dma_start(out=out[t * P:(t + 1) * P, n * 512:(n + 1) * 512],
-                                  in_=res.rearrange("p r c -> p (r c)"))
+            c0 = CHUNKS[k // 2] * 512 + k % 2 * 256
+            nt, t0 = len(tiles), tiles[0]
+            pa, pb = prods[k, t0]
+            e = eng[t0]
+            (nc.vector if e == "v" else nc.gpsimd).tensor_tensor(out=pa[:], in0=pa[:], in1=pb[:], op=ALU.add)
+            nc.sync.dma_start(out=out[t0 * P:(t0 + nt) * P, c0:c0 + 256].rearrange("(t p) c -> p t c", t=nt),
+                              in_=pa[:].rearrange("p t r c -> p t (r c)"))
 
-        PAIRS = ((0, 1), (2, 3))
         HA, HB = H_ORDER
+        XO, WO = OPT["xout"], OPT["w0out"]
+        for t, eng in OPT["turn_head"]:
+            count_turns(t, eng)
+        for t, eng in OPT["turn_head"]:
+            take_turns(t)
         prepare(("x", 0), x_sb[0], KH)
         x_turn(0, HA)
         x_turn(0, HB)
-        keep_clock(2)
-        run(tables_half(0, 0))
+        keep_clock(OPT["d1"])
+        if OPT["tabhead"] == 2:
+            run(tables_half(0, 0))
         x_out(0, HA, "s")
         x_out(0, HB, "v")
         prepare(("w", 0), w_sb[0], 2 * KH)
-        w_turn(0, HA)
-        w_out(0, HA, "sv")
-        x_quant(0)
-        keep_clock(2)
-        w_turn(0, HB)
-        keep_clock(2)
         prepare(("x", 1), x_sb[1], KH)
-        w_out(0, HB, "sv")
+        w_turn(0, HA)
+        w_out(0, HA, WO)
+        x_quant(0)
+        keep_clock(OPT["d2"])
+        w_turn(0, HB)
+        keep_clock(OPT["d3"])
+        if OPT["tabhead"] == 1:
+            run(tables_half(0, 0))
+        w_out(0, HB, WO)
+        prepare(("x", 2), x_sb[2], KH)
         w_quant(0, HA)
         x_turn(1, HA)
         x_turn(1, HB)
-        keep_clock(2)
-        prepare(("x", 2), x_sb[2], KH)
-        x_out(1, HA, "s")
-        x_out(1, HB, "v")
+        keep_clock(OPT["d4"])
+        x_out(1, HA, XO[0])
+        x_out(1, HB, XO[1])
         w_quant(0, HB)
         x_turn(2, HA)
         x_turn(2, HB)
-        keep_clock(2)
+        keep_clock(OPT["d5"])
         prepare(("x", 3), x_sb[3], KH)
-        x_out(2, HA, "s")
-        x_out(2, HB, "v")
+        x_out(2, HA, XO[0])
+        x_out(2, HB, XO[1])
         x_quant(1)
         x_turn(3, HA)
         x_turn(3, HB)
-        keep_clock(2)
         prepare(("w", 1), w_sb[1], 2 * KH)
-        x_out(3, HA, "s")
-        x_out(3, HB, "v")
+        x_out(3, HA, XO[0])
+        x_out(3, HB, XO[1])
         x_quant(2)
-        x_quant(3)
+        if OPT["tabhead"] == 0:
+            run(tables_half(0, 0))
         run(tables_half(0, 1))
-        turned = []
-        multiplied = []
-        waiting = [(0, PAIRS[0]), (0, PAIRS[1])]
+        passes = [(k, t) for k in range(NU) for t in range(NT)]
 
-        def vector_step():
+        def multiply_next(n):
+            for i in range(n):
+                multiply(*passes.pop(0))
+
+        def quantise_turned():
             while turned:
                 w_quant(*turned.pop(0))
-            while multiplied:
-                k0, tiles = multiplied.pop(0)
-                products(k0, tiles)
-                if k0 % 2 == 1:
-                    add_store(k0, tiles, "g")
 
+        def rotate_next():
+            k0, tiles = multiplied.pop(0)
+            products(k0, tiles)
+            if True:
+                add_store(k0, tiles, OPT["addk"].get(k0, OPT["addlast" if k0 == NU - 1 else "add"]))
+
+        def rotate_all():
+            while multiplied:
+                rotate_next()
+
+        multiply_next(OPT["m0"][0])
+        x3 = [3]
+        due = []
         for k in range(1, NU):
             calls = tables_half((k + 1) // 2, (k + 1) % 2)
             cut = len(calls) // 2
             for i, h in enumerate(H_ORDER):
                 w_turn(k, h)
-                w_out(k, h, "ss")
-                vector_step()
+                w_out(k, h, OPT["wouts"])
+                while due:
+                    take_turns(due.pop(0))
+                while x3:
+                    x_quant(x3.pop(0))
+                if OPT["qfirst"] and (k, i) != (NU - 1, 1):
+                    quantise_turned()
+                    rotate_all()
+                else:
+                    rotate_all()
+                    quantise_turned()
                 turned.append((k, h))
                 if i == 0:
                     if k + 1 < NU:
                         prepare(("w", k + 1), w_sb[k + 1], 2 * KH)
                     for t in TURNS_AT.get(k, ()):
-                        reduce_turns(t)
+                        if t not in [z for z, q in OPT["turn_head"]]:
+                            count_turns(t, OPT["turn_eng"])
+                            due.append(t)
+                    if not OPT["turn_lag"]:
+                        while due:
+                            take_turns(due.pop(0))
                     run(calls[:cut])
                 else:
                     run(calls[cut:])
-                if (k, i) == (1, 0):
-                    keep_clock(2)
-                else:
-                    k0, tiles = waiting.pop(0)
-                    multiply(k0, tiles)
-                    multiplied.append((k0, tiles))
-            waiting += [(k, (t,)) for t in range(NT)] if k >= NU - 1 else [(k, PAIRS[0]), (k, PAIRS[1])]
-        vector_step()
-        for k0, tiles in waiting:
-            multiply(k0, tiles)
-            products(k0, tiles)
-            if k0 % 2 == 1:
-                add_store(k0, tiles, "g" if tiles[0] < 2 else "v")
+                multiply_next(OPT["mc"][2 * (k - 1) + i])
+        for i in range(OPT["rq"]):
+            rotate_next()
+        quantise_turned()
+        rotate_all()
+        while passes:
+            multiply_next(1)
+            rotate_all()

import math
from contextlib import ExitStack

import concourse.mybir as mybir
from concourse.masks import make_identity

F32 = mybir.dt.float32
BF16 = mybir.dt.bfloat16
I32 = mybir.dt.int32
U32 = mybir.dt.uint32
U8 = mybir.dt.uint8
FP8X4 = mybir.dt.float8_e4m3fn_x4
ALU = mybir.AluOpType
ACT = mybir.ActivationFunctionType

P = 128
S, D = 512, 2048
HALF = D // 2
BASE = 10000.0
FLOPS = 2 * S * D * D

NT = S // P
NG = D // 512
NU = 8
KH = D // 2
H_ORDER = (0, 1)
TWO_PI = 2.0 * math.pi
THR = (496, 576)
CHUNKS = (3, 2, 1, 0)
PERM_H = ()
TURNS_AT = {1: (2, 3), 2: (0, 1)}
OPT = {"turn_eng": 's', "turn_head": ((2, 's'), (3, 's')), "turn_lag": 1, "neg": 'v', "xout": 'sv', "perm": {(('x', 2), 0): 'v', (('x', 2), 1): 'v'}, "add": 'gggg', "addlast": 'gvgv', "d0": 4, "d1": 2, "d2": 1, "d3": 2, "d4": 2, "d5": 0, "m0": (1,), "mc": (1, 1, 1, 2, 2, 2, 2, 2, 2, 2, 2, 2, 2, 2), "addk": {}, "qfirst": True, "w0out": 'ss', "tabhead": 1, "wouts": 'ss', "rq": 0, "pb": 4, "single": 7}


def tile_ropeattention_pa_kernel(tc, x, w, out):
    nc = tc.nc
    with ExitStack() as ctx:
        const = ctx.enter_context(tc.tile_pool(name="const", bufs=1))
        big = ctx.enter_context(tc.tile_pool(name="big", bufs=1))
        grp = ctx.enter_context(tc.tile_pool(name="grp", bufs=5))
        codes = ctx.enter_context(tc.tile_pool(name="codes", bufs=3))
        perm = ctx.enter_context(tc.tile_pool(name="perm", bufs=2))
        work = ctx.enter_context(tc.tile_pool(name="work", bufs=3))
        psum = ctx.enter_context(tc.psum_pool(name="psum", bufs=4))
        ctx.enter_context(tc.manual_schedule())

        x_sb = [[big.tile([P, KH], BF16, name="x_sb%d_%d" % (t, h)) for h in range(2)] for t in range(NT)]
        w_sb = [[big.tile([P, 2 * KH], BF16, name="w_sb%d_%d" % (k, h)) for h in range(2)] for k in range(NU)]

        def load_x(t):
            for h in H_ORDER:
                nc.sync.dma_start(out=x_sb[t][h][:], in_=x[t * P:(t + 1) * P, h * KH:(h + 1) * KH])

        def load_w(k):
            c0 = CHUNKS[k // 2] * 512 + k % 2 * 256
            rows = w[c0:c0 + 256, :].rearrange("(p e) k -> p e k", e=2)
            for h in H_ORDER:
                nc.sync.dma_start(out=w_sb[k][h][:].rearrange("p (e k) -> p e k", e=2),
                                  in_=rows[:, :, h * KH:(h + 1) * KH])

        load_x(0)
        load_w(0)
        for t in range(1, NT):
            load_x(t)
        for k in range(1, NU):
            load_w(k)

        zeros = const.tile([P, 512], BF16, name="zeros")
        nc.vector.memset(zeros[:].bitcast(I32), 0)

        def keep_clock(n):
            idle = psum.tile([P, 512], F32, name="y")
            for i in range(n):
                nc.tensor.matmul(idle[:], lhsT=zeros[:, 0:P], rhs=zeros[:], start=True, stop=True)

        keep_clock(OPT["d0"])
        warm = const.tile([P, 2], F32, name="warm")
        nc.vector.memset(warm[:, 0:1], 0.0)
        nc.scalar.activation(out=warm[:, 1:2], in_=warm[:, 0:1], func=ACT.Sin)
        s_int = const.tile([P, NT], I32, name="s_int")
        nc.gpsimd.iota(s_int[:], pattern=[[P, NT]], base=0, channel_multiplier=1)
        ident = const.tile([P, P], F32, name="ident")
        make_identity(nc, ident[:])
        sc = const.tile([P, 16], F32, name="sc")
        freq = const.tile([P, HALF], F32, name="freq")
        nc.vector.memset(freq[:, 0:1], 1.0)
        nc.vector.memset(sc[:, 12:13], 1.0)
        nc.vector.tensor_copy(out=sc[:, 0:4], in_=s_int[:])
        nc.vector.tensor_scalar(out=sc[:, 8:12], in0=sc[:, 0:4], scalar1=1.0 / TWO_PI, scalar2=None, op0=ALU.mult)
        size = 1
        while size < HALF:
            for m in range(1, 4):
                nc.vector.tensor_scalar(
                    out=freq[:, m * size:(m + 1) * size], in0=freq[:, 0:size],
                    scalar1=BASE ** (-(m * size) / HALF), scalar2=None, op0=ALU.mult,
                )
            size *= 4
        nc.vector.tensor_scalar(out=sc[:, 4:8], in0=sc[:, 0:4], scalar1=-1.0, scalar2=None, op0=ALU.mult)
        nc.vector.tensor_scalar(out=sc[:, 13:14], in0=sc[:, 12:13], scalar1=0.5 * math.pi, scalar2=None, op0=ALU.mult)
        half_pi = sc[:, 13:14]

        frac = [const.tile([P, 2, THR[tp]], F32, name="frac%d" % tp) for tp in range(2)]
        afr = [const.tile([P, 2, THR[tp]], F32, name="afr%d" % tp) for tp in range(2)]
        tab = [const.tile([P, NT, 3, 256], F32, name="tab%d" % n) for n in range(4)]

        turns_of = {}

        def count_turns(t, eng):
            hi = THR[t // 2]
            turns_of[t] = work.tile([P, 576], I32, name="turns", bufs=2)
            if eng == "g":
                nc.gpsimd.tensor_scalar(out=turns_of[t][:, 0:hi], in0=freq[:, 0:hi], scalar1=sc[:, 8 + t:9 + t],
                                        scalar2=0.0, op0=ALU.mult, op1=ALU.add)
            else:
                nc.scalar.activation(out=turns_of[t][:, 0:hi].bitcast(U32), in_=freq[:, 0:hi], func=ACT.Copy,
                                     scale=sc[:, 8 + t:9 + t])

        def take_turns(t):
            hi = THR[t // 2]
            nc.vector.scalar_tensor_tensor(out=frac[t // 2][:, t % 2, :], in0=freq[:, 0:hi], scalar=sc[:, 8 + t:9 + t],
                                           in1=turns_of[t][:, 0:hi], op0=ALU.mult, op1=ALU.subtract)

        def tables_half(c, tp):
            calls = []
            if c >= len(CHUNKS):
                return calls
            n = CHUNKS[c]
            lo, hi = 256 * n, 256 * (n + 1)
            mid = min(max(THR[tp], lo), hi)
            both = slice(2 * tp, 2 * tp + 2)
            if mid > lo:
                calls.append(lambda: nc.scalar.activation(
                    out=afr[tp][:, :, lo:mid], in_=frac[tp][:, :, lo:mid], func=ACT.Abs))
                calls.append(lambda: nc.scalar.activation(
                    out=tab[n][:, both, 2, 0:mid - lo], in_=frac[tp][:, :, lo:mid], func=ACT.Sin, scale=TWO_PI))
                calls.append(lambda: nc.scalar.activation(
                    out=tab[n][:, both, 1, 0:mid - lo], in_=afr[tp][:, :, lo:mid], func=ACT.Sin,
                    scale=-TWO_PI, bias=half_pi))
            if mid < hi:
                for t in (2 * tp, 2 * tp + 1):
                    calls.append(lambda t=t: nc.scalar.activation(
                        out=tab[n][:, t, 2, mid - lo:256], in_=freq[:, mid:hi], func=ACT.Sin, scale=sc[:, t:t + 1]))
                    calls.append(lambda t=t: nc.scalar.activation(
                        out=tab[n][:, t, 1, mid - lo:256], in_=freq[:, mid:hi], func=ACT.Sin,
                        scale=sc[:, 4 + t:5 + t], bias=half_pi))
            if OPT["neg"] == "s":
                if mid > lo:
                    calls.append(lambda: nc.scalar.activation(
                        out=tab[n][:, both, 0, 0:mid - lo], in_=frac[tp][:, :, lo:mid], func=ACT.Sin, scale=-TWO_PI))
                if mid < hi:
                    for t in (2 * tp, 2 * tp + 1):
                        calls.append(lambda t=t: nc.scalar.activation(
                            out=tab[n][:, t, 0, mid - lo:256], in_=freq[:, mid:hi], func=ACT.Sin, scale=sc[:, 4 + t:5 + t]))
            elif OPT["neg"] == "v":
                calls.append(lambda: nc.vector.tensor_scalar(
                    out=tab[n][:, both, 0, :], in0=tab[n][:, both, 2, :], scalar1=-1.0, scalar2=None, op0=ALU.mult))
            else:
                calls.append(lambda: nc.gpsimd.tensor_scalar(
                    out=tab[n][:, both, 0, :], in0=tab[n][:, both, 2, :],
                    scalar1=-1.0, scalar2=0.0, op0=ALU.mult, op1=ALU.add))
            return calls

        def run(calls):
            for call in calls:
                call()

        x_codes = [big.tile([P, 512], U32, name="x_codes%d" % t, align_bytes=64) for t in range(NT)]
        x_scale = [big.tile([P, 512], U8, name="x_scale%d" % t, align_bytes=64) for t in range(NT)]

        def copy_out(eng, dst, src):
            if eng == "v":
                nc.vector.tensor_copy(out=dst, in_=src)
            else:
                nc.scalar.copy(out=dst, in_=src)

        def regroup(raw, na, engs):
            out_t = perm.tile([P, 2 * KH], BF16, name="perm")
            src = raw[:].bitcast(F32).rearrange("p (a c u) -> p a u c", a=na, u=2)
            dst = out_t[:, 0:na * KH].bitcast(F32).rearrange("p (a u c) -> p a u c", a=na, u=2)
            for a in range(na):
                copy_out(engs[a], dst[:, a], src[:, a])
            return out_t

        ready = {}

        def prepare(key, raw, n):
            for h in H_ORDER:
                engs = OPT["perm"].get((key, h))
                ready[key, h] = (regroup(raw[h], n // KH, engs) if engs else raw[h])[:].bitcast(F32)

        def columns(words, key, a, gl, u, na):
            if key in OPT["perm"]:
                c0 = a * 512 + u * 256 + gl * P
                return words[:, c0:c0 + P]
            c0 = a * 512 + gl * 2 * P
            return words[:, c0 + u:c0 + 2 * P:2]

        x_g4 = {}
        pend = {}

        def x_turn(t, h):
            words = ready[("x", t), h]
            bank = psum.tile([P, 512], F32, name="tp")
            for gl in range(2):
                for u in range(2):
                    nc.tensor.transpose(bank[:, (2 * gl + u) * P:(2 * gl + u + 1) * P],
                                        columns(words, (("x", t), h), 0, gl, u, 1), ident[:])
            pend["x", t, h] = bank

        def x_out(t, h, eng):
            if t not in x_g4:
                x_g4[t] = grp.tile([P, 2048], BF16, name="g4", align_bytes=64)
            bank = pend["x", t, h]
            copy_out(eng, x_g4[t][:].bitcast(F32)[:, h * 512:(h + 1) * 512].rearrange("p (g r u) -> p g r u", g=2, u=2),
                     bank[:].rearrange("p (g u r) -> p g r u", g=2, u=2))

        def x_quant(t):
            nc.vector.quantize_mx(out=x_codes[t][:].bitcast(FP8X4), scales=x_scale[t][:], in_=x_g4[t][:])

        w_codes = {}
        w_scale = {}
        w_g4 = {}

        def w_turn(k, h):
            words = ready[("w", k), h]
            for gl in range(2):
                bank = psum.tile([P, 512], F32, name="tp")
                for u in range(2):
                    for a in range(2):
                        nc.tensor.transpose(bank[:, (2 * u + a) * P:(2 * u + a + 1) * P],
                                            columns(words, (("w", k), h), a, gl, u, 2), ident[:])
                pend[k, h, gl] = bank

        def w_out(k, h, engs):
            g4 = grp.tile([P, 2048], BF16, name="g4", align_bytes=64)
            w_g4[k, h] = g4
            g4w = g4[:].bitcast(F32)
            for gl in range(2):
                copy_out(engs[gl], g4w[:, gl * 512:(gl + 1) * 512].rearrange("p (c u) -> p c u", u=2),
                         pend[k, h, gl][:].rearrange("p (u c) -> p c u", u=2))

        def w_quant(k, h):
            if k not in w_codes:
                w_codes[k] = codes.tile([P, 1024], U32, name="w_codes", align_bytes=64)
                w_scale[k] = codes.tile([P, 1024], U8, name="w_scale", align_bytes=64)
            nc.vector.quantize_mx(out=w_codes[k][:, h * 512:(h + 1) * 512].bitcast(FP8X4),
                                  scales=w_scale[k][:, h * 512:(h + 1) * 512], in_=w_g4[k, h][:])

        prods = {}
        banks = {}
        turned = []
        multiplied = []

        def multiply(k, t):
            j = 0 if k >= OPT["single"] else t % 2
            if j == 0:
                banks[k, t] = psum.tile([P, 512], F32, name="tp" if k == NU - 1 else "y")
            y = banks[k, t - j]
            for g in range(NG):
                nc.tensor.matmul_mx(
                    out=y[:, j * 256:(j + 1) * 256],
                    lhsT=x_codes[t][:, g * P:(g + 1) * P].bitcast(FP8X4),
                    lhsT_scale=x_scale[t][:, g * P:(g + 1) * P],
                    rhs=w_codes[k][:, g * 256:(g + 1) * 256].bitcast(FP8X4),
                    rhs_scale=w_scale[k][:, g * 256:(g + 1) * 256],
                    start=(g == 0), stop=(g == NG - 1),
                )
            if k >= OPT["single"]:
                multiplied.append((k, (t,)))
            elif j == 1:
                multiplied.append((k, (t - 1, t)))

        def products(k, tiles):
            n, r0 = CHUNKS[k // 2], k % 2 * P
            nt = len(tiles)
            y = banks[k, tiles[0]]
            ye = y[:, 0:nt * 256].rearrange("p (t e r) -> p t e r", t=nt, e=2)
            prods[k, tiles[0]] = [work.tile([P, nt, P, 2], F32, name="p%d_%d" % (e, nt), bufs=OPT["pb"]) for e in range(2)]
            for e in range(2):
                nc.vector.tensor_tensor(
                    out=prods[k, tiles[0]][e][:],
                    in0=ye[:, :, e, :].unsqueeze(3).to_broadcast([P, nt, P, 2]),
                    in1=tab[n][:, tiles[0]:tiles[0] + nt, 1 - e:3 - e, r0:r0 + P].rearrange("p t c r -> p t r c"),
                    op=ALU.mult,
                )

        def add_store(k, tiles, eng):
            c0 = CHUNKS[k // 2] * 512 + k % 2 * 256
            nt, t0 = len(tiles), tiles[0]
            pa, pb = prods[k, t0]
            e = eng[t0]
            (nc.vector if e == "v" else nc.gpsimd).tensor_tensor(out=pa[:], in0=pa[:], in1=pb[:], op=ALU.add)
            nc.sync.dma_start(out=out[t0 * P:(t0 + nt) * P, c0:c0 + 256].rearrange("(t p) c -> p t c", t=nt),
                              in_=pa[:].rearrange("p t r c -> p t (r c)"))

        HA, HB = H_ORDER
        XO, WO = OPT["xout"], OPT["w0out"]
        for t, eng in OPT["turn_head"]:
            count_turns(t, eng)
        for t, eng in OPT["turn_head"]:
            take_turns(t)
        prepare(("x", 0), x_sb[0], KH)
        x_turn(0, HA)
        x_turn(0, HB)
        keep_clock(OPT["d1"])
        if OPT["tabhead"] == 2:
            run(tables_half(0, 0))
        x_out(0, HA, "s")
        x_out(0, HB, "v")
        prepare(("w", 0), w_sb[0], 2 * KH)
        prepare(("x", 1), x_sb[1], KH)
        w_turn(0, HA)
        w_out(0, HA, WO)
        x_quant(0)
        keep_clock(OPT["d2"])
        w_turn(0, HB)
        keep_clock(OPT["d3"])
        if OPT["tabhead"] == 1:
            run(tables_half(0, 0))
        w_out(0, HB, WO)
        prepare(("x", 2), x_sb[2], KH)
        w_quant(0, HA)
        x_turn(1, HA)
        x_turn(1, HB)
        keep_clock(OPT["d4"])
        x_out(1, HA, XO[0])
        x_out(1, HB, XO[1])
        w_quant(0, HB)
        x_turn(2, HA)
        x_turn(2, HB)
        keep_clock(OPT["d5"])
        prepare(("x", 3), x_sb[3], KH)
        x_out(2, HA, XO[0])
        x_out(2, HB, XO[1])
        x_quant(1)
        x_turn(3, HA)
        x_turn(3, HB)
        prepare(("w", 1), w_sb[1], 2 * KH)
        x_out(3, HA, XO[0])
        x_out(3, HB, XO[1])
        x_quant(2)
        if OPT["tabhead"] == 0:
            run(tables_half(0, 0))
        run(tables_half(0, 1))
        passes = [(k, t) for k in range(NU) for t in range(NT)]

        def multiply_next(n):
            for i in range(n):
                multiply(*passes.pop(0))

        def quantise_turned():
            while turned:
                w_quant(*turned.pop(0))

        def rotate_next():
            k0, tiles = multiplied.pop(0)
            products(k0, tiles)
            if True:
                add_store(k0, tiles, OPT["addk"].get(k0, OPT["addlast" if k0 == NU - 1 else "add"]))

        def rotate_all():
            while multiplied:
                rotate_next()

        multiply_next(OPT["m0"][0])
        x3 = [3]
        due = []
        for k in range(1, NU):
            calls = tables_half((k + 1) // 2, (k + 1) % 2)
            cut = len(calls) // 2
            for i, h in enumerate(H_ORDER):
                w_turn(k, h)
                w_out(k, h, OPT["wouts"])
                while due:
                    take_turns(due.pop(0))
                while x3:
                    x_quant(x3.pop(0))
                if OPT["qfirst"] and (k, i) != (NU - 1, 1):
                    quantise_turned()
                    rotate_all()
                else:
                    rotate_all()
                    quantise_turned()
                turned.append((k, h))
                if i == 0:
                    if k + 1 < NU:
                        prepare(("w", k + 1), w_sb[k + 1], 2 * KH)
                    for t in TURNS_AT.get(k, ()):
                        if t not in [z for z, q in OPT["turn_head"]]:
                            count_turns(t, OPT["turn_eng"])
                            due.append(t)
                    if not OPT["turn_lag"]:
                        while due:
                            take_turns(due.pop(0))
                    run(calls[:cut])
                else:
                    run(calls[cut:])
                multiply_next(OPT["mc"][2 * (k - 1) + i])
        for i in range(OPT["rq"]):
            rotate_next()
        quantise_turned()
        rotate_all()
        while passes:
            multiply_next(1)
            rotate_all()
